import numpy as np
import ml_dtypes


def mxq(x, axis, fmt="e4m3"):
    dtype, down = {"e4m3": (ml_dtypes.float8_e4m3fn, 7), "e5m2": (ml_dtypes.float8_e5m2, 14)}[fmt]
    v = np.moveaxis(np.asarray(x, np.float32).astype(ml_dtypes.bfloat16).astype(np.float64), axis, -1)
    blocks = v.reshape(v.shape[:-1] + (-1, 32))
    amax = np.abs(blocks).max(-1, keepdims=True)
    byte = np.maximum(np.where(amax > 0, np.frexp(amax)[1] - 1 + 127, 0) - down, 1)
    scale = np.exp2(byte - 127.0)
    codes = (blocks / scale).astype(np.float32).astype(dtype).astype(np.float64)
    return np.moveaxis((codes * scale).reshape(v.shape), -1, axis)


WIDE = False


def mx_kscale(k):
    if not WIDE:
        return np.ones(k)
    levels = np.array([10, -10, 5, -5, 0])
    a = np.random.permutation(np.resize(levels, k // 512 * 4)).reshape(k // 512, 4)
    idx = np.arange(k)
    return np.exp2(a[idx // 512, idx % 128 // 32])


BF16 = ml_dtypes.bfloat16


def bf(x):
    return np.asarray(x, np.float32).astype(BF16)


def f64(x):
    return np.asarray(x).astype(np.float64)


E2M1 = np.array([0.0, 0.5, 1.0, 1.5, 2.0, 3.0, 4.0, 6.0, -0.0, -0.5, -1.0, -1.5, -2.0, -3.0, -4.0, -6.0])


def pack_weight(w, fmt):
    k, n = w.shape
    w = f64(bf(w)).reshape(k // 32, 32, n)
    amax = np.abs(w).max(1)
    if fmt == "e4m3":
        byte = np.frexp(amax)[1] - 1 + 127 - 7
    else:
        mant, ex = np.frexp(amax / 6.0)
        byte = np.where(mant > 0.5, ex, ex - 1) + 127
    byte = np.clip(np.where(amax > 0, byte, 1), 1, 254)
    scaled = (w * np.exp2(127.0 - byte)[:, None, :]).reshape(k, n).astype(np.float32)
    by_word = np.ascontiguousarray(scaled.reshape(k // 512, 128, 4, n).transpose(0, 1, 3, 2))
    if fmt == "e4m3":
        words = by_word.astype(ml_dtypes.float8_e4m3fn).view(np.uint8)
    else:
        c = by_word.astype(ml_dtypes.float4_e2m1fn).view(np.uint8) & 0xF
        words = c[..., 0::2] | (c[..., 1::2] << 4)
    return np.ascontiguousarray(words), np.ascontiguousarray(byte.astype(np.uint8).reshape(k // 512, 16, n))


def unpack_weight(words, scales, fmt):
    g, p, n, _ = words.shape
    if fmt == "e4m3":
        vals = np.ascontiguousarray(words).view(ml_dtypes.float8_e4m3fn).astype(np.float64)
    else:
        nib = np.empty((g, p, n, 4), np.uint8)
        nib[..., 0::2] = words & 0xF
        nib[..., 1::2] = words >> 4
        vals = E2M1[nib]
    vals = vals * np.repeat(np.exp2(scales.astype(np.float64) - 127.0), 8, axis=1)[..., None]
    return vals.transpose(0, 1, 3, 2).reshape(g * 512, n)


B, S, HID, NH, DH = 4, 256, 1024, 16, 64
DQ = NH * DH
FMT = "e4m3"


def setup_inputs():
    s = mx_kscale(HID)

    def w():
        return pack_weight(np.random.standard_normal((HID, DQ)) / np.sqrt(HID) / s[:, None], FMT)

    def b():
        return bf(np.random.standard_normal(DQ) * 0.3)

    x = bf(np.random.standard_normal((B, S, HID)) * s)
    reasoning_mask = bf(np.random.uniform(size=(B, S, 1, 1)))
    Wq_words, Wq_scales = w()
    bq = b()
    Wk_words, Wk_scales = w()
    bk = b()
    Wqr_words, Wqr_scales = w()
    bqr = b()
    Wkr_words, Wkr_scales = w()
    bkr = b()
    return {"x": x,
            "reasoning_mask": reasoning_mask,
            "Wq_words": Wq_words, "Wq_scales": Wq_scales, "bq": bq,
            "Wk_words": Wk_words, "Wk_scales": Wk_scales, "bk": bk,
            "Wqr_words": Wqr_words, "Wqr_scales": Wqr_scales, "bqr": bqr,
            "Wkr_words": Wkr_words, "Wkr_scales": Wkr_scales, "bkr": bkr}


def reference(x, reasoning_mask, Wq_words, Wq_scales, bq, Wk_words, Wk_scales, bk, Wqr_words, Wqr_scales, bqr, Wkr_words, Wkr_scales, bkr):
    xq = mxq(f64(x), 2, "e4m3")
    g = f64(reasoning_mask)

    def proj(words, scales, b):
        return ((xq @ unpack_weight(words, scales, FMT)) + f64(b)).reshape(B, S, NH, DH)

    q = proj(Wq_words, Wq_scales, bq)
    k = proj(Wk_words, Wk_scales, bk)
    q_r = proj(Wqr_words, Wqr_scales, bqr)
    k_r = proj(Wkr_words, Wkr_scales, bkr)
    q = q * (1.0 - g) + q_r * g
    k = k * (1.0 - g) + k_r * g
    return q, k

@@ -1,0 +1,248 @@
+from contextlib import ExitStack
+
+import concourse.mybir as mybir
+from concourse.masks import make_identity
+
+F32 = mybir.dt.float32
+BF16 = mybir.dt.bfloat16
+I32 = mybir.dt.int32
+U32 = mybir.dt.uint32
+U8 = mybir.dt.uint8
+FP8X4 = mybir.dt.float8_e4m3fn_x4
+MULT = mybir.AluOpType.mult
+ADD = mybir.AluOpType.add
+COPY = mybir.ActivationFunctionType.Copy
+
+P = 128
+TOKENS = 1024
+HID = 1024
+DQ = 1024
+TILES = TOKENS // P
+PACK = 4
+K_PASS = P * PACK
+PASSES = HID // K_PASS
+WORDS = 2
+PASS_WORDS = K_PASS // 2
+N_BLOCK = 512
+SIDES = 2
+BLOCKS_PER_SIDE = DQ // N_BLOCK
+COL_BLOCKS = SIDES * BLOCKS_PER_SIDE
+PAIR = 2
+ROUNDS_PER_BLOCK = TILES // PAIR
+ROUNDS = COL_BLOCKS * ROUNDS_PER_BLOCK
+PLAIN, REASONING = 0, 1
+QUADRANTS = 4
+SCALE_ROWS = 4
+AHEAD = 2
+
+FLOPS = 4 * 2 * TOKENS * HID * DQ
+
+
+def tile_reasoningmultiheadattention_pa_kernel(
+    tc, x, reasoning_mask,
+    Wq_words, Wq_scales, bq, Wk_words, Wk_scales, bk,
+    Wqr_words, Wqr_scales, bqr, Wkr_words, Wkr_scales, bkr,
+    out_0, out_1,
+):
+    nc = tc.nc
+    words_in = ((Wq_words, Wqr_words), (Wk_words, Wkr_words))
+    scales_in = ((Wq_scales, Wqr_scales), (Wk_scales, Wkr_scales))
+    bias_in = ((bq, bqr), (bk, bkr))
+    outs = (out_0, out_1)
+
+    x_view = x.rearrange("b s k -> (b s) k").rearrange("(p a) k -> p a k", a=TILES)
+    gate_view = reasoning_mask.rearrange("b s o i -> (b s) (o i)").rearrange("(p a) o -> p (a o)", a=TILES)
+    out_views = [
+        o.rearrange("b s h d -> (b s) (h d)").rearrange("(p a) n -> p a n", a=TILES) for o in outs
+    ]
+
+    with ExitStack() as ctx:
+        ctx.enter_context(tc.manual_schedule())
+        keep = ctx.enter_context(tc.tile_pool(name="keep", bufs=1))
+        stream = ctx.enter_context(tc.tile_pool(name="stream", bufs=2))
+        psum = ctx.enter_context(tc.psum_pool(name="psum", bufs=8))
+
+        ident = keep.tile([P, P], F32, name="ident")
+        gate_bf = keep.tile([P, TILES], BF16, name="gate_bf")
+        gate = keep.tile([P, TILES], F32, name="gate")
+        one_minus_gate = keep.tile([P, TILES], F32, name="one_minus_gate")
+        pick_plain = keep.tile([P, P], BF16, name="pick_plain")
+        pick_diff = keep.tile([P, P], BF16, name="pick_diff")
+        bias_rows = [keep.tile([P, DQ], BF16, name="bias_rows%d" % s) for s in range(SIDES)]
+        plain_bias = keep.tile([P, COL_BLOCKS, N_BLOCK], F32, name="plain_bias")
+        x_raw = [keep.tile([P, PAIR, HID], BF16, name="x_raw%d" % j) for j in range(ROUNDS_PER_BLOCK)]
+        x_codes = keep.tile([P, TILES, PASSES * P], U32, name="x_codes", align_bytes=64)
+        x_scales = keep.tile([P, TILES, PASSES * P], U8, name="x_scales", align_bytes=64)
+        w_words = [
+            [keep.tile([P, PASSES, DQ], U32, name="w_words%d%d" % (s, w), align_bytes=64) for w in range(2)]
+            for s in range(SIDES)
+        ]
+        w_planes = [keep.tile([P, DQ], U8, name="w_planes%d" % s, align_bytes=64) for s in range(SIDES)]
+
+        for s in range(SIDES):
+            nc.vector.memset(w_planes[s][:].bitcast(I32), 0)
+            nc.vector.memset(bias_rows[s][:], 0.0)
+        nc.vector.memset(pick_plain[:], 0.0)
+        nc.vector.memset(pick_plain[0:1, :], 1.0)
+        nc.vector.memset(pick_diff[:], 0.0)
+        nc.vector.memset(pick_diff[0:1, :], -1.0)
+        nc.vector.memset(pick_diff[32:33, :], 1.0)
+        make_identity(nc, ident[:])
+
+        def load_bias_rows(s):
+            for w in range(2):
+                nc.sync.dma_start(
+                    out=bias_rows[s][32 * w : 32 * w + 1, :],
+                    in_=bias_in[s][w].rearrange("(o n) -> o n", o=1),
+                )
+
+        def load_scales(s, w):
+            rows = PASSES * SCALE_ROWS
+            for quad in range(QUADRANTS):
+                first = 32 * quad + rows * w
+                nc.sync.dma_start(
+                    out=w_planes[s][first : first + rows, :].bitcast(I32),
+                    in_=scales_in[s][w][:, SCALE_ROWS * quad : SCALE_ROWS * (quad + 1), :].bitcast(I32),
+                )
+
+        def load_words(c, w):
+            s, b = divmod(c, BLOCKS_PER_SIDE)
+            cols = slice(b * N_BLOCK, (b + 1) * N_BLOCK)
+            nc.sync.dma_start(
+                out=w_words[s][w][:, :, cols].bitcast(I32),
+                in_=words_in[s][w].rearrange("g p n t -> p g (n t)").bitcast(I32)[:, :, cols],
+            )
+
+        def load_x(j):
+            nc.sync.dma_start(out=x_raw[j][:], in_=x_view[:, PAIR * j : PAIR * (j + 1), :])
+
+        nc.sync.dma_start(out=gate_bf[:], in_=gate_view)
+        load_bias_rows(0)
+        load_scales(0, PLAIN)
+        load_x(0)
+        load_words(0, PLAIN)
+        load_scales(0, REASONING)
+        load_words(0, REASONING)
+        for j in range(1, ROUNDS_PER_BLOCK):
+            load_x(j)
+        load_bias_rows(1)
+        load_words(1, PLAIN)
+        load_words(1, REASONING)
+        load_scales(1, PLAIN)
+        load_scales(1, REASONING)
+        for c in range(BLOCKS_PER_SIDE, COL_BLOCKS):
+            load_words(c, PLAIN)
+            load_words(c, REASONING)
+
+        nc.vector.tensor_copy(out=gate[:], in_=gate_bf[:])
+        nc.vector.tensor_scalar(
+            out=one_minus_gate[:], in0=gate[:], scalar1=-1.0, scalar2=1.0, op0=MULT, op1=ADD
+        )
+
+        diff_banks = {}
+
+        def spread_bias(c):
+            s, b = divmod(c, BLOCKS_PER_SIDE)
+            cols = slice(b * N_BLOCK, (b + 1) * N_BLOCK)
+            diff_bank = psum.tile([P, N_BLOCK], F32, tag="bank", name="diff_bank")
+            nc.tensor.matmul(out=diff_bank[:], lhsT=pick_diff[:], rhs=bias_rows[s][:, cols], start=True, stop=True)
+            diff_banks[c] = diff_bank
+            plain_bank = psum.tile([P, N_BLOCK], F32, tag="bank", name="plain_bank")
+            nc.tensor.matmul(out=plain_bank[:], lhsT=pick_plain[:], rhs=bias_rows[s][:, cols], start=True, stop=True)
+            nc.scalar.copy(out=plain_bias[:, c, :], in_=plain_bank[:])
+
+        def blend_bias(r):
+            c, j = divmod(r, ROUNDS_PER_BLOCK)
+            bias = stream.tile([P, PAIR, N_BLOCK], F32, name="bias", bufs=8)
+            for i in range(PAIR):
+                a = PAIR * j + i
+                if c == 0:
+                    nc.vector.scalar_tensor_tensor(
+                        out=bias[:, i, :], in0=diff_banks[c][:], scalar=gate[:, a : a + 1],
+                        in1=plain_bias[:, c, :], op0=MULT, op1=ADD,
+                    )
+                else:
+                    nc.scalar.activation(
+                        out=bias[:, i, :], in_=diff_banks[c][:], func=COPY, scale=gate[:, a : a + 1]
+                    )
+            if c > 0:
+                nc.gpsimd.tensor_tensor(
+                    out=bias[:], in0=bias[:],
+                    in1=plain_bias[:, c, :].unsqueeze(1).to_broadcast([P, PAIR, N_BLOCK]), op=ADD,
+                )
+            return bias
+
+        def prepare_x(a):
+            words = x_raw[a // PAIR][:, a % PAIR, :].bitcast(F32)
+            flipped = psum.tile([P, PASSES, WORDS, P], F32, tag="bank", name="flipped")
+            for g in range(PASSES):
+                for u in range(WORDS):
+                    nc.tensor.transpose(
+                        flipped[:, g, u, :],
+                        words[:, PASS_WORDS * g + u : PASS_WORDS * (g + 1) : WORDS],
+                        ident[:],
+                    )
+            grouped = stream.tile([P, PASSES * P * PACK], BF16, name="grouped", align_bytes=64)
+            nc.scalar.copy(
+                out=grouped[:].bitcast(F32).rearrange("p (g r u) -> p g r u", g=PASSES, u=WORDS),
+                in_=flipped[:].rearrange("p g u r -> p g r u"),
+            )
+            nc.vector.quantize_mx(
+                out=x_codes[:, a, :].bitcast(FP8X4), scales=x_scales[:, a, :], in_=grouped[:]
+            )
+
+        def project(c, a, w):
+            s, b = divmod(c, BLOCKS_PER_SIDE)
+            cols = slice(b * N_BLOCK, (b + 1) * N_BLOCK)
+            bank = psum.tile([P, N_BLOCK], F32, tag="bank", name="bank")
+            for g in range(PASSES):
+                tokens = slice(g * P, (g + 1) * P)
+                first_row = SCALE_ROWS * (PASSES * w + g)
+                nc.tensor.matmul_mx(
+                    out=bank[:],
+                    lhsT=x_codes[:, a, tokens].bitcast(FP8X4),
+                    lhsT_scale=x_scales[:, a, tokens],
+                    rhs=w_words[s][w][:, g, cols].bitcast(FP8X4),
+                    rhs_scale=w_planes[s][first_row:P, cols],
+                    start=(g == 0),
+                    stop=(g == PASSES - 1),
+                )
+            return bank
+
+        spread_bias(0)
+        biases = {}
+        for r in range(AHEAD):
+            biases[r] = blend_bias(r)
+        for a in range(PAIR):
+            prepare_x(a)
+
+        for r in range(ROUNDS):
+            c, j = divmod(r, ROUNDS_PER_BLOCK)
+            s, b = divmod(c, BLOCKS_PER_SIDE)
+            cols = slice(b * N_BLOCK, (b + 1) * N_BLOCK)
+            tiles = range(PAIR * j, PAIR * (j + 1))
+            if j == 0 and c + 1 < COL_BLOCKS:
+                spread_bias(c + 1)
+            if r + AHEAD < ROUNDS:
+                biases[r + AHEAD] = blend_bias(r + AHEAD)
+
+            parts = {}
+            for a in tiles:
+                bank = project(c, a, PLAIN)
+                part = stream.tile([P, N_BLOCK], F32, name="part", bufs=4)
+                nc.vector.scalar_tensor_tensor(
+                    out=part[:], in0=bank[:], scalar=one_minus_gate[:, a : a + 1],
+                    in1=biases[r][:, a % PAIR, :], op0=MULT, op1=ADD,
+                )
+                parts[a] = part
+            if c == 0 and j + 1 < ROUNDS_PER_BLOCK:
+                for a in tiles:
+                    prepare_x(a + PAIR)
+            for a in tiles:
+                bank = project(c, a, REASONING)
+                result = stream.tile([P, N_BLOCK], F32, name="result", bufs=8)
+                nc.vector.scalar_tensor_tensor(
+                    out=result[:], in0=bank[:], scalar=gate[:, a : a + 1],
+                    in1=parts[a][:], op0=MULT, op1=ADD,
+                )
+                nc.sync.dma_start(out=out_views[s][:, a, cols], in_=result[:])

@@ -33,7 +33,8 @@ ROUNDS = COL_BLOCKS * ROUNDS_PER_BLOCK
 PLAIN, REASONING = 0, 1
 QUADRANTS = 4
 SCALE_ROWS = 4
-AHEAD = 2
+HEAD_ROUNDS = 2
+AHEAD = 3
 
 FLOPS = 4 * 2 * TOKENS * HID * DQ
 
@@ -70,7 +71,8 @@ def tile_reasoningmultiheadattention_pa_kernel(
         pick_diff = keep.tile([P, P], BF16, name="pick_diff")
         bias_rows = [keep.tile([P, DQ], BF16, name="bias_rows%d" % s) for s in range(SIDES)]
         plain_bias = keep.tile([P, COL_BLOCKS, N_BLOCK], F32, name="plain_bias")
-        x_raw = [keep.tile([P, PAIR, HID], BF16, name="x_raw%d" % j) for j in range(ROUNDS_PER_BLOCK)]
+        bias_diff = keep.tile([P, COL_BLOCKS, N_BLOCK], F32, name="bias_diff")
+        x_raw = [keep.tile([P, HID], BF16, name="x_raw%d" % a) for a in range(TILES)]
         x_codes = keep.tile([P, TILES, PASSES * P], U32, name="x_codes", align_bytes=64)
         x_scales = keep.tile([P, TILES, PASSES * P], U8, name="x_scales", align_bytes=64)
         w_words = [
@@ -113,19 +115,20 @@ def tile_reasoningmultiheadattention_pa_kernel(
                 in_=words_in[s][w].rearrange("g p n t -> p g (n t)").bitcast(I32)[:, :, cols],
             )
 
-        def load_x(j):
-            nc.sync.dma_start(out=x_raw[j][:], in_=x_view[:, PAIR * j : PAIR * (j + 1), :])
+        def load_x(a):
+            nc.sync.dma_start(out=x_raw[a][:], in_=x_view[:, a, :])
 
+        load_x(0)
         nc.sync.dma_start(out=gate_bf[:], in_=gate_view)
         load_bias_rows(0)
         load_scales(0, PLAIN)
-        load_x(0)
         load_words(0, PLAIN)
+        load_x(1)
         load_scales(0, REASONING)
         load_words(0, REASONING)
-        for j in range(1, ROUNDS_PER_BLOCK):
-            load_x(j)
         load_bias_rows(1)
+        for a in range(PAIR, TILES):
+            load_x(a)
         load_words(1, PLAIN)
         load_words(1, REASONING)
         load_scales(1, PLAIN)
@@ -139,33 +142,31 @@ def tile_reasoningmultiheadattention_pa_kernel(
             out=one_minus_gate[:], in0=gate[:], scalar1=-1.0, scalar2=1.0, op0=MULT, op1=ADD
         )
 
-        diff_banks = {}
-
         def spread_bias(c):
             s, b = divmod(c, BLOCKS_PER_SIDE)
             cols = slice(b * N_BLOCK, (b + 1) * N_BLOCK)
             diff_bank = psum.tile([P, N_BLOCK], F32, tag="bank", name="diff_bank")
             nc.tensor.matmul(out=diff_bank[:], lhsT=pick_diff[:], rhs=bias_rows[s][:, cols], start=True, stop=True)
-            diff_banks[c] = diff_bank
+            nc.scalar.copy(out=bias_diff[:, c, :], in_=diff_bank[:])
             plain_bank = psum.tile([P, N_BLOCK], F32, tag="bank", name="plain_bank")
             nc.tensor.matmul(out=plain_bank[:], lhsT=pick_plain[:], rhs=bias_rows[s][:, cols], start=True, stop=True)
             nc.scalar.copy(out=plain_bias[:, c, :], in_=plain_bank[:])
 
         def blend_bias(r):
             c, j = divmod(r, ROUNDS_PER_BLOCK)
-            bias = stream.tile([P, PAIR, N_BLOCK], F32, name="bias", bufs=8)
+            bias = stream.tile([P, PAIR, N_BLOCK], F32, name="bias", bufs=ROUNDS)
             for i in range(PAIR):
                 a = PAIR * j + i
-                if c == 0:
+                if r < HEAD_ROUNDS:
                     nc.vector.scalar_tensor_tensor(
-                        out=bias[:, i, :], in0=diff_banks[c][:], scalar=gate[:, a : a + 1],
+                        out=bias[:, i, :], in0=bias_diff[:, c, :], scalar=gate[:, a : a + 1],
                         in1=plain_bias[:, c, :], op0=MULT, op1=ADD,
                     )
                 else:
                     nc.scalar.activation(
-                        out=bias[:, i, :], in_=diff_banks[c][:], func=COPY, scale=gate[:, a : a + 1]
+                        out=bias[:, i, :], in_=bias_diff[:, c, :], func=COPY, scale=gate[:, a : a + 1]
                     )
-            if c > 0:
+            if r >= HEAD_ROUNDS:
                 nc.gpsimd.tensor_tensor(
                     out=bias[:], in0=bias[:],
                     in1=plain_bias[:, c, :].unsqueeze(1).to_broadcast([P, PAIR, N_BLOCK]), op=ADD,
@@ -173,7 +174,7 @@ def tile_reasoningmultiheadattention_pa_kernel(
             return bias
 
         def prepare_x(a):
-            words = x_raw[a // PAIR][:, a % PAIR, :].bitcast(F32)
+            words = x_raw[a][:].bitcast(F32)
             flipped = psum.tile([P, PASSES, WORDS, P], F32, tag="bank", name="flipped")
             for g in range(PASSES):
                 for u in range(WORDS):
@@ -209,22 +210,21 @@ def tile_reasoningmultiheadattention_pa_kernel(
                 )
             return bank
 
-        spread_bias(0)
         biases = {}
-        for r in range(AHEAD):
+        prepare_x(0)
+        spread_bias(0)
+        biases[0] = blend_bias(0)
+        prepare_x(1)
+        for r in range(1, AHEAD):
             biases[r] = blend_bias(r)
-        for a in range(PAIR):
-            prepare_x(a)
 
         for r in range(ROUNDS):
             c, j = divmod(r, ROUNDS_PER_BLOCK)
             s, b = divmod(c, BLOCKS_PER_SIDE)
             cols = slice(b * N_BLOCK, (b + 1) * N_BLOCK)
             tiles = range(PAIR * j, PAIR * (j + 1))
-            if j == 0 and c + 1 < COL_BLOCKS:
-                spread_bias(c + 1)
-            if r + AHEAD < ROUNDS:
-                biases[r + AHEAD] = blend_bias(r + AHEAD)
+            if r + 1 < COL_BLOCKS:
+                spread_bias(r + 1)
 
             parts = {}
             for a in tiles:
@@ -238,6 +238,8 @@ def tile_reasoningmultiheadattention_pa_kernel(
             if c == 0 and j + 1 < ROUNDS_PER_BLOCK:
                 for a in tiles:
                     prepare_x(a + PAIR)
+            if r + AHEAD < ROUNDS:
+                biases[r + AHEAD] = blend_bias(r + AHEAD)
             for a in tiles:
                 bank = project(c, a, REASONING)
                 result = stream.tile([P, N_BLOCK], F32, name="result", bufs=8)

@@ -34,7 +34,8 @@ PLAIN, REASONING = 0, 1
 QUADRANTS = 4
 SCALE_ROWS = 4
 HEAD_ROUNDS = 2
-AHEAD = 3
+AHEAD = 4
+SPREAD_LAST_IN = 2
 
 FLOPS = 4 * 2 * TOKENS * HID * DQ
 
@@ -82,8 +83,9 @@ def tile_reasoningmultiheadattention_pa_kernel(
         w_planes = [keep.tile([P, DQ], U8, name="w_planes%d" % s, align_bytes=64) for s in range(SIDES)]
 
         for s in range(SIDES):
-            nc.vector.memset(w_planes[s][:].bitcast(I32), 0)
             nc.vector.memset(bias_rows[s][:], 0.0)
+        for s in range(SIDES):
+            nc.vector.memset(w_planes[s][:].bitcast(I32), 0)
         nc.vector.memset(pick_plain[:], 0.0)
         nc.vector.memset(pick_plain[0:1, :], 1.0)
         nc.vector.memset(pick_diff[:], 0.0)
@@ -93,7 +95,7 @@ def tile_reasoningmultiheadattention_pa_kernel(
 
         def load_bias_rows(s):
             for w in range(2):
-                nc.sync.dma_start(
+                nc.scalar.dma_start(
                     out=bias_rows[s][32 * w : 32 * w + 1, :],
                     in_=bias_in[s][w].rearrange("(o n) -> o n", o=1),
                 )
@@ -118,15 +120,15 @@ def tile_reasoningmultiheadattention_pa_kernel(
         def load_x(a):
             nc.sync.dma_start(out=x_raw[a][:], in_=x_view[:, a, :])
 
-        load_x(0)
-        nc.sync.dma_start(out=gate_bf[:], in_=gate_view)
         load_bias_rows(0)
+        nc.scalar.dma_start(out=gate_bf[:], in_=gate_view)
+        load_bias_rows(1)
+        load_x(0)
+        load_x(1)
         load_scales(0, PLAIN)
         load_words(0, PLAIN)
-        load_x(1)
         load_scales(0, REASONING)
         load_words(0, REASONING)
-        load_bias_rows(1)
         for a in range(PAIR, TILES):
             load_x(a)
         load_words(1, PLAIN)
@@ -147,10 +149,16 @@ def tile_reasoningmultiheadattention_pa_kernel(
             cols = slice(b * N_BLOCK, (b + 1) * N_BLOCK)
             diff_bank = psum.tile([P, N_BLOCK], F32, tag="bank", name="diff_bank")
             nc.tensor.matmul(out=diff_bank[:], lhsT=pick_diff[:], rhs=bias_rows[s][:, cols], start=True, stop=True)
-            nc.scalar.copy(out=bias_diff[:, c, :], in_=diff_bank[:])
             plain_bank = psum.tile([P, N_BLOCK], F32, tag="bank", name="plain_bank")
             nc.tensor.matmul(out=plain_bank[:], lhsT=pick_plain[:], rhs=bias_rows[s][:, cols], start=True, stop=True)
-            nc.scalar.copy(out=plain_bias[:, c, :], in_=plain_bank[:])
+            return diff_bank, plain_bank
+
+        def keep_bias(c, banks, plain_by_vector):
+            nc.scalar.copy(out=bias_diff[:, c, :], in_=banks[0][:])
+            if plain_by_vector:
+                nc.vector.tensor_copy(out=plain_bias[:, c, :], in_=banks[1][:])
+            else:
+                nc.scalar.copy(out=plain_bias[:, c, :], in_=banks[1][:])
 
         def blend_bias(r):
             c, j = divmod(r, ROUNDS_PER_BLOCK)
@@ -173,7 +181,7 @@ def tile_reasoningmultiheadattention_pa_kernel(
                 )
             return bias
 
-        def prepare_x(a):
+        def flip_x(a):
             words = x_raw[a][:].bitcast(F32)
             flipped = psum.tile([P, PASSES, WORDS, P], F32, tag="bank", name="flipped")
             for g in range(PASSES):
@@ -183,11 +191,17 @@ def tile_reasoningmultiheadattention_pa_kernel(
                         words[:, PASS_WORDS * g + u : PASS_WORDS * (g + 1) : WORDS],
                         ident[:],
                     )
-            grouped = stream.tile([P, PASSES * P * PACK], BF16, name="grouped", align_bytes=64)
+            return flipped
+
+        def group_x(flipped):
+            grouped = stream.tile([P, PASSES * P * PACK], BF16, name="grouped", align_bytes=64, bufs=4)
             nc.scalar.copy(
                 out=grouped[:].bitcast(F32).rearrange("p (g r u) -> p g r u", g=PASSES, u=WORDS),
                 in_=flipped[:].rearrange("p g u r -> p g r u"),
             )
+            return grouped
+
+        def quantise_x(a, grouped):
             nc.vector.quantize_mx(
                 out=x_codes[:, a, :].bitcast(FP8X4), scales=x_scales[:, a, :], in_=grouped[:]
             )
@@ -210,41 +224,65 @@ def tile_reasoningmultiheadattention_pa_kernel(
                 )
             return bank
 
+        def first_half(r, a):
+            c = r // ROUNDS_PER_BLOCK
+            bank = project(c, a, PLAIN)
+            part = stream.tile([P, N_BLOCK], F32, name="part", bufs=4)
+            return bank, part
+
+        def blend_plain(r, a, bank, part):
+            nc.vector.scalar_tensor_tensor(
+                out=part[:], in0=bank[:], scalar=one_minus_gate[:, a : a + 1],
+                in1=biases[r][:, a % PAIR, :], op0=MULT, op1=ADD,
+            )
+
+        def second_half(r, a, part):
+            c = r // ROUNDS_PER_BLOCK
+            s, b = divmod(c, BLOCKS_PER_SIDE)
+            cols = slice(b * N_BLOCK, (b + 1) * N_BLOCK)
+            bank = project(c, a, REASONING)
+            result = stream.tile([P, N_BLOCK], F32, name="result", bufs=12)
+            nc.vector.scalar_tensor_tensor(
+                out=result[:], in0=bank[:], scalar=gate[:, a : a + 1],
+                in1=part[:], op0=MULT, op1=ADD,
+            )
+            nc.sync.dma_start(out=out_views[s][:, a, cols], in_=result[:])
+
         biases = {}
-        prepare_x(0)
-        spread_bias(0)
+        flipped0 = flip_x(0)
+        banks0 = spread_bias(0)
+        grouped0 = group_x(flipped0)
+        quantise_x(0, grouped0)
+        keep_bias(0, banks0, True)
+        flipped1 = flip_x(1)
+        grouped1 = group_x(flipped1)
+        quantise_x(1, grouped1)
+        banks1 = spread_bias(1)
+        keep_bias(1, banks1, False)
         biases[0] = blend_bias(0)
-        prepare_x(1)
-        for r in range(1, AHEAD):
+        for r in range(HEAD_ROUNDS, AHEAD):
             biases[r] = blend_bias(r)
 
         for r in range(ROUNDS):
-            c, j = divmod(r, ROUNDS_PER_BLOCK)
-            s, b = divmod(c, BLOCKS_PER_SIDE)
-            cols = slice(b * N_BLOCK, (b + 1) * N_BLOCK)
+            j = r % ROUNDS_PER_BLOCK
             tiles = range(PAIR * j, PAIR * (j + 1))
-            if r + 1 < COL_BLOCKS:
-                spread_bias(r + 1)
-
+            if r == SPREAD_LAST_IN:
+                keep_bias(COL_BLOCKS - 1, spread_bias(COL_BLOCKS - 1), False)
             parts = {}
             for a in tiles:
-                bank = project(c, a, PLAIN)
-                part = stream.tile([P, N_BLOCK], F32, name="part", bufs=4)
-                nc.vector.scalar_tensor_tensor(
-                    out=part[:], in0=bank[:], scalar=one_minus_gate[:, a : a + 1],
-                    in1=biases[r][:, a % PAIR, :], op0=MULT, op1=ADD,
-                )
+                bank, part = first_half(r, a)
+                blend_plain(r, a, bank, part)
                 parts[a] = part
-            if c == 0 and j + 1 < ROUNDS_PER_BLOCK:
-                for a in tiles:
-                    prepare_x(a + PAIR)
             if r + AHEAD < ROUNDS:
                 biases[r + AHEAD] = blend_bias(r + AHEAD)
             for a in tiles:
-                bank = project(c, a, REASONING)
-                result = stream.tile([P, N_BLOCK], F32, name="result", bufs=8)
-                nc.vector.scalar_tensor_tensor(
-                    out=result[:], in0=bank[:], scalar=gate[:, a : a + 1],
-                    in1=parts[a][:], op0=MULT, op1=ADD,
-                )
-                nc.sync.dma_start(out=out_views[s][:, a, cols], in_=result[:])
+                second_half(r, a, parts[a])
+            if r == 0:
+                biases[1] = blend_bias(1)
+                flips = {}
+                for a in range(PAIR, TILES):
+                    if a == TILES - PAIR:
+                        banks2 = spread_bias(2)
+                    flips[a] = flip_x(a)
+                    quantise_x(a, group_x(flips[a]))
+                keep_bias(2, banks2, False)

@@ -35,7 +35,8 @@ QUADRANTS = 4
 SCALE_ROWS = 4
 HEAD_ROUNDS = 2
 AHEAD = 4
-SPREAD_LAST_IN = 2
+LAST_WIDTHS = (256, 128, 128)
+LONG_RUN = 4
 
 FLOPS = 4 * 2 * TOKENS * HID * DQ
 
@@ -70,9 +71,10 @@ def tile_reasoningmultiheadattention_pa_kernel(
         one_minus_gate = keep.tile([P, TILES], F32, name="one_minus_gate")
         pick_plain = keep.tile([P, P], BF16, name="pick_plain")
         pick_diff = keep.tile([P, P], BF16, name="pick_diff")
-        bias_rows = [keep.tile([P, DQ], BF16, name="bias_rows%d" % s) for s in range(SIDES)]
-        plain_bias = keep.tile([P, COL_BLOCKS, N_BLOCK], F32, name="plain_bias")
-        bias_diff = keep.tile([P, COL_BLOCKS, N_BLOCK], F32, name="bias_diff")
+        bias_rows = keep.tile([P, DQ], BF16, name="bias_rows")
+        plain_bias = keep.tile([P, BLOCKS_PER_SIDE, N_BLOCK], F32, name="plain_bias")
+        bias_diff = keep.tile([P, BLOCKS_PER_SIDE, N_BLOCK], F32, name="bias_diff")
+        spread = [keep.tile([P, DQ], BF16, name="spread%d" % w) for w in range(2)]
         x_raw = [keep.tile([P, HID], BF16, name="x_raw%d" % a) for a in range(TILES)]
         x_codes = keep.tile([P, TILES, PASSES * P], U32, name="x_codes", align_bytes=64)
         x_scales = keep.tile([P, TILES, PASSES * P], U8, name="x_scales", align_bytes=64)
@@ -82,8 +84,7 @@ def tile_reasoningmultiheadattention_pa_kernel(
         ]
         w_planes = [keep.tile([P, DQ], U8, name="w_planes%d" % s, align_bytes=64) for s in range(SIDES)]
 
-        for s in range(SIDES):
-            nc.vector.memset(bias_rows[s][:], 0.0)
+        nc.vector.memset(bias_rows[:], 0.0)
         for s in range(SIDES):
             nc.vector.memset(w_planes[s][:].bitcast(I32), 0)
         nc.vector.memset(pick_plain[:], 0.0)
@@ -93,11 +94,11 @@ def tile_reasoningmultiheadattention_pa_kernel(
         nc.vector.memset(pick_diff[32:33, :], 1.0)
         make_identity(nc, ident[:])
 
-        def load_bias_rows(s):
+        def load_bias_rows():
             for w in range(2):
-                nc.scalar.dma_start(
-                    out=bias_rows[s][32 * w : 32 * w + 1, :],
-                    in_=bias_in[s][w].rearrange("(o n) -> o n", o=1),
+                nc.sync.dma_start(
+                    out=bias_rows[32 * w : 32 * w + 1, :],
+                    in_=bias_in[0][w].rearrange("(o n) -> o n", o=1),
                 )
 
         def load_scales(s, w):
@@ -120,11 +121,10 @@ def tile_reasoningmultiheadattention_pa_kernel(
         def load_x(a):
             nc.sync.dma_start(out=x_raw[a][:], in_=x_view[:, a, :])
 
-        load_bias_rows(0)
-        nc.scalar.dma_start(out=gate_bf[:], in_=gate_view)
-        load_bias_rows(1)
         load_x(0)
         load_x(1)
+        load_bias_rows()
+        nc.sync.dma_start(out=gate_bf[:], in_=gate_view)
         load_scales(0, PLAIN)
         load_words(0, PLAIN)
         load_scales(0, REASONING)
@@ -133,6 +133,8 @@ def tile_reasoningmultiheadattention_pa_kernel(
             load_x(a)
         load_words(1, PLAIN)
         load_words(1, REASONING)
+        for w in range(2):
+            nc.sync.dma_start(out=spread[w][:], in_=bias_in[1][w].partition_broadcast(P))
         load_scales(1, PLAIN)
         load_scales(1, REASONING)
         for c in range(BLOCKS_PER_SIDE, COL_BLOCKS):
@@ -148,9 +150,9 @@ def tile_reasoningmultiheadattention_pa_kernel(
             s, b = divmod(c, BLOCKS_PER_SIDE)
             cols = slice(b * N_BLOCK, (b + 1) * N_BLOCK)
             diff_bank = psum.tile([P, N_BLOCK], F32, tag="bank", name="diff_bank")
-            nc.tensor.matmul(out=diff_bank[:], lhsT=pick_diff[:], rhs=bias_rows[s][:, cols], start=True, stop=True)
+            nc.tensor.matmul(out=diff_bank[:], lhsT=pick_diff[:], rhs=bias_rows[:, cols], start=True, stop=True)
             plain_bank = psum.tile([P, N_BLOCK], F32, tag="bank", name="plain_bank")
-            nc.tensor.matmul(out=plain_bank[:], lhsT=pick_plain[:], rhs=bias_rows[s][:, cols], start=True, stop=True)
+            nc.tensor.matmul(out=plain_bank[:], lhsT=pick_plain[:], rhs=bias_rows[:, cols], start=True, stop=True)
             return diff_bank, plain_bank
 
         def keep_bias(c, banks, plain_by_vector):
@@ -163,6 +165,19 @@ def tile_reasoningmultiheadattention_pa_kernel(
         def blend_bias(r):
             c, j = divmod(r, ROUNDS_PER_BLOCK)
             bias = stream.tile([P, PAIR, N_BLOCK], F32, name="bias", bufs=ROUNDS)
+            if c >= BLOCKS_PER_SIDE:
+                cols = slice((c - BLOCKS_PER_SIDE) * N_BLOCK, (c - BLOCKS_PER_SIDE + 1) * N_BLOCK)
+                other = stream.tile([P, PAIR, N_BLOCK], F32, name="other", bufs=3)
+                for i in range(PAIR):
+                    a = PAIR * j + i
+                    nc.scalar.activation(
+                        out=bias[:, i, :], in_=spread[PLAIN][:, cols], func=COPY, scale=one_minus_gate[:, a : a + 1]
+                    )
+                    nc.scalar.activation(
+                        out=other[:, i, :], in_=spread[REASONING][:, cols], func=COPY, scale=gate[:, a : a + 1]
+                    )
+                nc.gpsimd.tensor_tensor(out=bias[:], in0=bias[:], in1=other[:], op=ADD)
+                return bias
             for i in range(PAIR):
                 a = PAIR * j + i
                 if r < HEAD_ROUNDS:
@@ -206,10 +221,10 @@ def tile_reasoningmultiheadattention_pa_kernel(
                 out=x_codes[:, a, :].bitcast(FP8X4), scales=x_scales[:, a, :], in_=grouped[:]
             )
 
-        def project(c, a, w):
+        def project(c, a, w, first=0, width=N_BLOCK):
             s, b = divmod(c, BLOCKS_PER_SIDE)
-            cols = slice(b * N_BLOCK, (b + 1) * N_BLOCK)
-            bank = psum.tile([P, N_BLOCK], F32, tag="bank", name="bank")
+            cols = slice(b * N_BLOCK + first, b * N_BLOCK + first + width)
+            bank = psum.tile([P, width], F32, tag="bank", name="bank")
             for g in range(PASSES):
                 tokens = slice(g * P, (g + 1) * P)
                 first_row = SCALE_ROWS * (PASSES * w + g)
@@ -236,26 +251,26 @@ def tile_reasoningmultiheadattention_pa_kernel(
                 in1=biases[r][:, a % PAIR, :], op0=MULT, op1=ADD,
             )
 
-        def second_half(r, a, part):
+        def second_half(r, a, part, first=0, width=N_BLOCK):
             c = r // ROUNDS_PER_BLOCK
             s, b = divmod(c, BLOCKS_PER_SIDE)
-            cols = slice(b * N_BLOCK, (b + 1) * N_BLOCK)
-            bank = project(c, a, REASONING)
-            result = stream.tile([P, N_BLOCK], F32, name="result", bufs=12)
+            cols = slice(b * N_BLOCK + first, b * N_BLOCK + first + width)
+            bank = project(c, a, REASONING, first, width)
+            result = stream.tile([P, width], F32, name="result", bufs=12)
             nc.vector.scalar_tensor_tensor(
                 out=result[:], in0=bank[:], scalar=gate[:, a : a + 1],
-                in1=part[:], op0=MULT, op1=ADD,
+                in1=part[:, first : first + width], op0=MULT, op1=ADD,
             )
             nc.sync.dma_start(out=out_views[s][:, a, cols], in_=result[:])
 
         biases = {}
         flipped0 = flip_x(0)
-        banks0 = spread_bias(0)
         grouped0 = group_x(flipped0)
         quantise_x(0, grouped0)
-        keep_bias(0, banks0, True)
         flipped1 = flip_x(1)
+        banks0 = spread_bias(0)
         grouped1 = group_x(flipped1)
+        keep_bias(0, banks0, True)
         quantise_x(1, grouped1)
         banks1 = spread_bias(1)
         keep_bias(1, banks1, False)
@@ -266,8 +281,6 @@ def tile_reasoningmultiheadattention_pa_kernel(
         for r in range(ROUNDS):
             j = r % ROUNDS_PER_BLOCK
             tiles = range(PAIR * j, PAIR * (j + 1))
-            if r == SPREAD_LAST_IN:
-                keep_bias(COL_BLOCKS - 1, spread_bias(COL_BLOCKS - 1), False)
             parts = {}
             for a in tiles:
                 bank, part = first_half(r, a)
@@ -276,13 +289,15 @@ def tile_reasoningmultiheadattention_pa_kernel(
             if r + AHEAD < ROUNDS:
                 biases[r + AHEAD] = blend_bias(r + AHEAD)
             for a in tiles:
-                second_half(r, a, parts[a])
+                if r == ROUNDS - 1 and a == TILES - 1:
+                    for i, width in enumerate(LAST_WIDTHS):
+                        second_half(r, a, parts[a], sum(LAST_WIDTHS[:i]), width)
+                else:
+                    second_half(r, a, parts[a])
             if r == 0:
                 biases[1] = blend_bias(1)
-                flips = {}
-                for a in range(PAIR, TILES):
-                    if a == TILES - PAIR:
-                        banks2 = spread_bias(2)
-                    flips[a] = flip_x(a)
-                    quantise_x(a, group_x(flips[a]))
-                keep_bias(2, banks2, False)
+                for a in range(PAIR, PAIR + LONG_RUN):
+                    quantise_x(a, group_x(flip_x(a)))
+            if r == 1:
+                for a in range(PAIR + LONG_RUN, TILES):
+                    quantise_x(a, group_x(flip_x(a)))

from contextlib import ExitStack

import concourse.mybir as mybir
from concourse.masks import make_identity

F32 = mybir.dt.float32
BF16 = mybir.dt.bfloat16
I32 = mybir.dt.int32
U32 = mybir.dt.uint32
U8 = mybir.dt.uint8
FP8X4 = mybir.dt.float8_e4m3fn_x4
MULT = mybir.AluOpType.mult
ADD = mybir.AluOpType.add
COPY = mybir.ActivationFunctionType.Copy

P = 128
TOKENS = 1024
HID = 1024
DQ = 1024
TILES = TOKENS // P
PACK = 4
K_PASS = P * PACK
PASSES = HID // K_PASS
WORDS = 2
PASS_WORDS = K_PASS // 2
N_BLOCK = 512
SIDES = 2
BLOCKS_PER_SIDE = DQ // N_BLOCK
COL_BLOCKS = SIDES * BLOCKS_PER_SIDE
PAIR = 2
ROUNDS_PER_BLOCK = TILES // PAIR
ROUNDS = COL_BLOCKS * ROUNDS_PER_BLOCK
PLAIN, REASONING = 0, 1
QUADRANTS = 4
SCALE_ROWS = 4
HEAD_ROUNDS = 2
AHEAD = 4
LAST_WIDTHS = (256, 128, 128)
LONG_RUN = 4

FLOPS = 4 * 2 * TOKENS * HID * DQ


def tile_reasoningmultiheadattention_pa_kernel(
    tc, x, reasoning_mask,
    Wq_words, Wq_scales, bq, Wk_words, Wk_scales, bk,
    Wqr_words, Wqr_scales, bqr, Wkr_words, Wkr_scales, bkr,
    out_0, out_1,
):
    nc = tc.nc
    words_in = ((Wq_words, Wqr_words), (Wk_words, Wkr_words))
    scales_in = ((Wq_scales, Wqr_scales), (Wk_scales, Wkr_scales))
    bias_in = ((bq, bqr), (bk, bkr))
    outs = (out_0, out_1)

    x_view = x.rearrange("b s k -> (b s) k").rearrange("(p a) k -> p a k", a=TILES)
    gate_view = reasoning_mask.rearrange("b s o i -> (b s) (o i)").rearrange("(p a) o -> p (a o)", a=TILES)
    out_views = [
        o.rearrange("b s h d -> (b s) (h d)").rearrange("(p a) n -> p a n", a=TILES) for o in outs
    ]

    with ExitStack() as ctx:
        ctx.enter_context(tc.manual_schedule())
        keep = ctx.enter_context(tc.tile_pool(name="keep", bufs=1))
        stream = ctx.enter_context(tc.tile_pool(name="stream", bufs=2))
        psum = ctx.enter_context(tc.psum_pool(name="psum", bufs=8))

        ident = keep.tile([P, P], F32, name="ident")
        gate_bf = keep.tile([P, TILES], BF16, name="gate_bf")
        gate = keep.tile([P, TILES], F32, name="gate")
        one_minus_gate = keep.tile([P, TILES], F32, name="one_minus_gate")
        pick_plain = keep.tile([P, P], BF16, name="pick_plain")
        pick_diff = keep.tile([P, P], BF16, name="pick_diff")
        bias_rows = keep.tile([P, DQ], BF16, name="bias_rows")
        plain_bias = keep.tile([P, BLOCKS_PER_SIDE, N_BLOCK], F32, name="plain_bias")
        bias_diff = keep.tile([P, BLOCKS_PER_SIDE, N_BLOCK], F32, name="bias_diff")
        spread = [keep.tile([P, DQ], BF16, name="spread%d" % w) for w in range(2)]
        x_raw = [keep.tile([P, HID], BF16, name="x_raw%d" % a) for a in range(TILES)]
        x_codes = keep.tile([P, TILES, PASSES * P], U32, name="x_codes", align_bytes=64)
        x_scales = keep.tile([P, TILES, PASSES * P], U8, name="x_scales", align_bytes=64)
        w_words = [
            [keep.tile([P, PASSES, DQ], U32, name="w_words%d%d" % (s, w), align_bytes=64) for w in range(2)]
            for s in range(SIDES)
        ]
        w_planes = [keep.tile([P, DQ], U8, name="w_planes%d" % s, align_bytes=64) for s in range(SIDES)]

        nc.vector.memset(bias_rows[:], 0.0)
        for s in range(SIDES):
            nc.vector.memset(w_planes[s][:].bitcast(I32), 0)
        nc.vector.memset(pick_plain[:], 0.0)
        nc.vector.memset(pick_plain[0:1, :], 1.0)
        nc.vector.memset(pick_diff[:], 0.0)
        nc.vector.memset(pick_diff[0:1, :], -1.0)
        nc.vector.memset(pick_diff[32:33, :], 1.0)
        make_identity(nc, ident[:])

        def load_bias_rows():
            for w in range(2):
                nc.sync.dma_start(
                    out=bias_rows[32 * w : 32 * w + 1, :],
                    in_=bias_in[0][w].rearrange("(o n) -> o n", o=1),
                )

        def load_scales(s, w):
            rows = PASSES * SCALE_ROWS
            for quad in range(QUADRANTS):
                first = 32 * quad + rows * w
                nc.sync.dma_start(
                    out=w_planes[s][first : first + rows, :].bitcast(I32),
                    in_=scales_in[s][w][:, SCALE_ROWS * quad : SCALE_ROWS * (quad + 1), :].bitcast(I32),
                )

        def load_words(c, w):
            s, b = divmod(c, BLOCKS_PER_SIDE)
            cols = slice(b * N_BLOCK, (b + 1) * N_BLOCK)
            nc.sync.dma_start(
                out=w_words[s][w][:, :, cols].bitcast(I32),
                in_=words_in[s][w].rearrange("g p n t -> p g (n t)").bitcast(I32)[:, :, cols],
            )

        def load_x(a):
            nc.sync.dma_start(out=x_raw[a][:], in_=x_view[:, a, :])

        load_x(0)
        load_x(1)
        load_bias_rows()
        nc.sync.dma_start(out=gate_bf[:], in_=gate_view)
        load_scales(0, PLAIN)
        load_words(0, PLAIN)
        load_scales(0, REASONING)
        load_words(0, REASONING)
        for a in range(PAIR, TILES):
            load_x(a)
        load_words(1, PLAIN)
        load_words(1, REASONING)
        for w in range(2):
            nc.sync.dma_start(out=spread[w][:], in_=bias_in[1][w].partition_broadcast(P))
        load_scales(1, PLAIN)
        load_scales(1, REASONING)
        for c in range(BLOCKS_PER_SIDE, COL_BLOCKS):
            load_words(c, PLAIN)
            load_words(c, REASONING)

        nc.vector.tensor_copy(out=gate[:], in_=gate_bf[:])
        nc.vector.tensor_scalar(
            out=one_minus_gate[:], in0=gate[:], scalar1=-1.0, scalar2=1.0, op0=MULT, op1=ADD
        )

        def spread_bias(c):
            s, b = divmod(c, BLOCKS_PER_SIDE)
            cols = slice(b * N_BLOCK, (b + 1) * N_BLOCK)
            diff_bank = psum.tile([P, N_BLOCK], F32, tag="bank", name="diff_bank")
            nc.tensor.matmul(out=diff_bank[:], lhsT=pick_diff[:], rhs=bias_rows[:, cols], start=True, stop=True)
            plain_bank = psum.tile([P, N_BLOCK], F32, tag="bank", name="plain_bank")
            nc.tensor.matmul(out=plain_bank[:], lhsT=pick_plain[:], rhs=bias_rows[:, cols], start=True, stop=True)
            return diff_bank, plain_bank

        def keep_bias(c, banks, plain_by_vector):
            nc.scalar.copy(out=bias_diff[:, c, :], in_=banks[0][:])
            if plain_by_vector:
                nc.vector.tensor_copy(out=plain_bias[:, c, :], in_=banks[1][:])
            else:
                nc.scalar.copy(out=plain_bias[:, c, :], in_=banks[1][:])

        def blend_bias(r):
            c, j = divmod(r, ROUNDS_PER_BLOCK)
            bias = stream.tile([P, PAIR, N_BLOCK], F32, name="bias", bufs=ROUNDS)
            if c >= BLOCKS_PER_SIDE:
                cols = slice((c - BLOCKS_PER_SIDE) * N_BLOCK, (c - BLOCKS_PER_SIDE + 1) * N_BLOCK)
                other = stream.tile([P, PAIR, N_BLOCK], F32, name="other", bufs=3)
                for i in range(PAIR):
                    a = PAIR * j + i
                    nc.scalar.activation(
                        out=bias[:, i, :], in_=spread[PLAIN][:, cols], func=COPY, scale=one_minus_gate[:, a : a + 1]
                    )
                    nc.scalar.activation(
                        out=other[:, i, :], in_=spread[REASONING][:, cols], func=COPY, scale=gate[:, a : a + 1]
                    )
                nc.gpsimd.tensor_tensor(out=bias[:], in0=bias[:], in1=other[:], op=ADD)
                return bias
            for i in range(PAIR):
                a = PAIR * j + i
                if r < HEAD_ROUNDS:
                    nc.vector.scalar_tensor_tensor(
                        out=bias[:, i, :], in0=bias_diff[:, c, :], scalar=gate[:, a : a + 1],
                        in1=plain_bias[:, c, :], op0=MULT, op1=ADD,
                    )
                else:
                    nc.scalar.activation(
                        out=bias[:, i, :], in_=bias_diff[:, c, :], func=COPY, scale=gate[:, a : a + 1]
                    )
            if r >= HEAD_ROUNDS:
                nc.gpsimd.tensor_tensor(
                    out=bias[:], in0=bias[:],
                    in1=plain_bias[:, c, :].unsqueeze(1).to_broadcast([P, PAIR, N_BLOCK]), op=ADD,
                )
            return bias

        def flip_x(a):
            words = x_raw[a][:].bitcast(F32)
            flipped = psum.tile([P, PASSES, WORDS, P], F32, tag="bank", name="flipped")
            for g in range(PASSES):
                for u in range(WORDS):
                    nc.tensor.transpose(
                        flipped[:, g, u, :],
                        words[:, PASS_WORDS * g + u : PASS_WORDS * (g + 1) : WORDS],
                        ident[:],
                    )
            return flipped

        def group_x(flipped):
            grouped = stream.tile([P, PASSES * P * PACK], BF16, name="grouped", align_bytes=64, bufs=4)
            nc.scalar.copy(
                out=grouped[:].bitcast(F32).rearrange("p (g r u) -> p g r u", g=PASSES, u=WORDS),
                in_=flipped[:].rearrange("p g u r -> p g r u"),
            )
            return grouped

        def quantise_x(a, grouped):
            nc.vector.quantize_mx(
                out=x_codes[:, a, :].bitcast(FP8X4), scales=x_scales[:, a, :], in_=grouped[:]
            )

        def project(c, a, w, first=0, width=N_BLOCK):
            s, b = divmod(c, BLOCKS_PER_SIDE)
            cols = slice(b * N_BLOCK + first, b * N_BLOCK + first + width)
            bank = psum.tile([P, width], F32, tag="bank", name="bank")
            for g in range(PASSES):
                tokens = slice(g * P, (g + 1) * P)
                first_row = SCALE_ROWS * (PASSES * w + g)
                nc.tensor.matmul_mx(
                    out=bank[:],
                    lhsT=x_codes[:, a, tokens].bitcast(FP8X4),
                    lhsT_scale=x_scales[:, a, tokens],
                    rhs=w_words[s][w][:, g, cols].bitcast(FP8X4),
                    rhs_scale=w_planes[s][first_row:P, cols],
                    start=(g == 0),
                    stop=(g == PASSES - 1),
                )
            return bank

        def first_half(r, a):
            c = r // ROUNDS_PER_BLOCK
            bank = project(c, a, PLAIN)
            part = stream.tile([P, N_BLOCK], F32, name="part", bufs=4)
            return bank, part

        def blend_plain(r, a, bank, part):
            nc.vector.scalar_tensor_tensor(
                out=part[:], in0=bank[:], scalar=one_minus_gate[:, a : a + 1],
                in1=biases[r][:, a % PAIR, :], op0=MULT, op1=ADD,
            )

        def second_half(r, a, part, first=0, width=N_BLOCK):
            c = r // ROUNDS_PER_BLOCK
            s, b = divmod(c, BLOCKS_PER_SIDE)
            cols = slice(b * N_BLOCK + first, b * N_BLOCK + first + width)
            bank = project(c, a, REASONING, first, width)
            result = stream.tile([P, width], F32, name="result", bufs=12)
            nc.vector.scalar_tensor_tensor(
                out=result[:], in0=bank[:], scalar=gate[:, a : a + 1],
                in1=part[:, first : first + width], op0=MULT, op1=ADD,
            )
            nc.sync.dma_start(out=out_views[s][:, a, cols], in_=result[:])

        biases = {}
        flipped0 = flip_x(0)
        grouped0 = group_x(flipped0)
        quantise_x(0, grouped0)
        flipped1 = flip_x(1)
        banks0 = spread_bias(0)
        grouped1 = group_x(flipped1)
        keep_bias(0, banks0, True)
        quantise_x(1, grouped1)
        banks1 = spread_bias(1)
        keep_bias(1, banks1, False)
        biases[0] = blend_bias(0)
        for r in range(HEAD_ROUNDS, AHEAD):
            biases[r] = blend_bias(r)

        for r in range(ROUNDS):
            j = r % ROUNDS_PER_BLOCK
            tiles = range(PAIR * j, PAIR * (j + 1))
            parts = {}
            for a in tiles:
                bank, part = first_half(r, a)
                blend_plain(r, a, bank, part)
                parts[a] = part
            if r + AHEAD < ROUNDS:
                biases[r + AHEAD] = blend_bias(r + AHEAD)
            for a in tiles:
                if r == ROUNDS - 1 and a == TILES - 1:
                    for i, width in enumerate(LAST_WIDTHS):
                        second_half(r, a, parts[a], sum(LAST_WIDTHS[:i]), width)
                else:
                    second_half(r, a, parts[a])
            if r == 0:
                biases[1] = blend_bias(1)
                for a in range(PAIR, PAIR + LONG_RUN):
                    quantise_x(a, group_x(flip_x(a)))
            if r == 1:
                for a in range(PAIR + LONG_RUN, TILES):
                    quantise_x(a, group_x(flip_x(a)))
